import numpy as np
import ml_dtypes


def mxq(x, axis, fmt="e4m3"):
    dtype, down = {"e4m3": (ml_dtypes.float8_e4m3fn, 7), "e5m2": (ml_dtypes.float8_e5m2, 14)}[fmt]
    v = np.moveaxis(np.asarray(x, np.float32).astype(ml_dtypes.bfloat16).astype(np.float64), axis, -1)
    blocks = v.reshape(v.shape[:-1] + (-1, 32))
    amax = np.abs(blocks).max(-1, keepdims=True)
    byte = np.maximum(np.where(amax > 0, np.frexp(amax)[1] - 1 + 127, 0) - down, 1)
    scale = np.exp2(byte - 127.0)
    codes = (blocks / scale).astype(np.float32).astype(dtype).astype(np.float64)
    return np.moveaxis((codes * scale).reshape(v.shape), -1, axis)


WIDE = False


def mx_kscale(k):
    if not WIDE:
        return np.ones(k)
    levels = np.array([10, -10, 5, -5, 0])
    if k % 512:
        return np.exp2(np.random.permutation(np.resize(levels, k // 32))).repeat(32)
    a = np.empty((k // 512, 16))
    for p in range(k // 512):
        a[p, :8] = np.random.permutation(np.resize(levels, 8))
        for g in range(8):
            far = levels[np.abs(levels - a[p, g]) >= 10]
            a[p, g + 8] = far[np.random.randint(len(far))]
    return np.exp2(a.ravel()).repeat(32)


BF16 = ml_dtypes.bfloat16


def bf(x):
    return np.asarray(x, np.float32).astype(BF16)


def f64(x):
    return np.asarray(x).astype(np.float64)


B, C, T, E, H = 1, 512, 4, 1024, 8
D = E // H
S = C * T


def heads(y):
    return np.moveaxis(y.reshape(B, C, T, H, D), 3, 1)


def setup_inputs():
    s = mx_kscale(E)
    return {"hidden_states": bf(np.random.standard_normal((B, S, E)) * s),
            "wk": bf(np.random.standard_normal((E, E)) * 2.0 / np.sqrt(E) / s[None, :]),
            "bk": bf(np.random.standard_normal(E) * 0.3),
            "wv": bf(np.random.standard_normal((E, E)) * 2.0 / np.sqrt(E) / s[None, :]),
            "bv": bf(np.random.standard_normal(E) * 0.3)}


def reference(hidden_states, wk, bk, wv, bv):
    xq = mxq(f64(hidden_states), 2, "e4m3")
    k = heads((xq @ mxq(f64(wk), 1, "e4m3").T) + f64(bk))
    v = heads((xq @ mxq(f64(wv), 1, "e4m3").T) + f64(bv))
    return k, v, k.mean(axis=3), v.mean(axis=3)

@@ -1,0 +1,204 @@
+from contextlib import ExitStack
+
+import concourse.mybir as mybir
+from concourse.masks import make_identity
+
+F32 = mybir.dt.float32
+BF16 = mybir.dt.bfloat16
+U32 = mybir.dt.uint32
+U8 = mybir.dt.uint8
+FP8X4 = mybir.dt.float8_e4m3fn_x4
+ADD = mybir.AluOpType.add
+MULT = mybir.AluOpType.mult
+COPY = mybir.ActivationFunctionType.Copy
+
+FLOPS = 2 * 2048 * 1024 * 2048
+
+P = 128
+BANK = 512
+UNIT = 4096
+WORDS = UNIT // 4
+ROUNDS = 16
+SCALE_LAG = 3
+
+
+def tile_chunkedattention_pb_kernel(tc, hidden_states, wk, bk, wv, bv, out_0, out_1, out_2, out_3):
+    nc = tc.nc
+    x_view = hidden_states.flatten_outer_dims().rearrange("(p q t) e -> p q (t e)", p=P, q=4, t=4)
+    w_views = [w.rearrange("(n f p) e -> p n f e", n=2, f=4, p=P) for w in (wk, wv)]
+    kv_views = [o.rearrange("b h (p q) t d -> p (b h) (q t d)", p=P, q=4) for o in (out_0, out_1)]
+    mean_views = [o.rearrange("b h (p q) d -> p (b h) (q d)", p=P, q=4) for o in (out_2, out_3)]
+
+    units = [("w", 0), ("x", 0), ("x", 1), ("x", 2), ("x", 3), ("w", 1), ("w", 2), ("w", 3)]
+
+    def first_round(unit):
+        kind, i = unit
+        return i if kind == "x" else 4 * i
+
+    def summed_on_vector(r):
+        return r % 4 == 3 and r > 3
+
+    with ExitStack() as ctx:
+        const = ctx.enter_context(tc.tile_pool(name="const", bufs=1))
+        raw_pool = ctx.enter_context(tc.tile_pool(name="raw_pool", bufs=4))
+        grouped_pool = ctx.enter_context(tc.tile_pool(name="grouped_pool", bufs=3))
+        out_pool = ctx.enter_context(tc.tile_pool(name="out_pool", bufs=8))
+        half_pool = ctx.enter_context(tc.tile_pool(name="half_pool", bufs=2))
+        total_pool = ctx.enter_context(tc.tile_pool(name="total_pool", bufs=SCALE_LAG + 2))
+        run_pool = ctx.enter_context(tc.tile_pool(name="run_pool", bufs=2))
+        mean_pool = ctx.enter_context(tc.tile_pool(name="mean_pool", bufs=2))
+        psum_t = ctx.enter_context(tc.psum_pool(name="psum_t", bufs=4))
+        psum_m = ctx.enter_context(tc.psum_pool(name="psum_m", bufs=4))
+        ctx.enter_context(tc.manual_schedule())
+
+        ident = const.tile([P, P], F32)
+        make_identity(nc, ident[:])
+        ones = const.tile([P, P], BF16)
+        nc.vector.memset(ones[:], 1.0)
+        bias_rows = const.tile([P, 4 * BANK], BF16)
+        nc.vector.memset(bias_rows[:], 0.0)
+        nc.scalar.dma_start(out=bias_rows[0:1, 0:2 * BANK], in_=bk.unsqueeze(0))
+        nc.scalar.dma_start(out=bias_rows[0:1, 2 * BANK:4 * BANK], in_=bv.unsqueeze(0))
+        bias = const.tile([P, 4 * BANK], F32)
+        codes = {
+            "x": const.tile([P, 4 * WORDS], U32, align_bytes=64, name="x_codes"),
+            "w": const.tile([P, 4 * WORDS], U32, align_bytes=64, name="w_codes"),
+        }
+        scales = {
+            "x": const.tile([P, 4 * WORDS], U8, align_bytes=64, name="x_scales"),
+            "w": const.tile([P, 4 * WORDS], U8, align_bytes=64, name="w_scales"),
+        }
+        raws = {}
+        groupeds = {}
+
+        def load(unit):
+            kind, i = unit
+            raw = raw_pool.tile([P, UNIT], BF16)
+            if kind == "x":
+                src = x_view[:, i, :].rearrange("p (f e) -> p f e", f=4)
+            else:
+                src = w_views[i // 2][:, i % 2]
+            dst = raw[:].rearrange("p (f e) -> p f e", f=4)
+            for f in (0, 2):
+                nc.sync.dma_start(out=dst[:, f:f + 2, :], in_=src[:, f:f + 2, :])
+            raws[unit] = raw
+
+        def transpose(unit, vector_helps):
+            kind = unit[0]
+            raw_words = raws[unit][:].bitcast(F32)
+            grouped = grouped_pool.tile([P, UNIT], BF16, align_bytes=64)
+            grouped_words = grouped[:].bitcast(F32)
+            if kind == "x":
+                dst = grouped_words.rearrange("p (f s c u) -> p f s c u", f=4, s=2, c=P, u=2)
+            else:
+                dst = grouped_words.rearrange("p (s f c u) -> p f s c u", s=2, f=4, c=P, u=2)
+            for f in range(4):
+                turned = psum_t.tile([P, BANK], F32)
+                for a in range(4):
+                    lo = BANK * f + 2 * P * (a // 2)
+                    nc.tensor.transpose(
+                        turned[:, P * a:P * (a + 1)], raw_words[:, lo + a % 2:lo + 2 * P:2], ident[:]
+                    )
+                src = turned[:].rearrange("p (s u c) -> p s c u", s=2, u=2, c=P)
+                if vector_helps and f % 2 == 1:
+                    nc.vector.tensor_copy(out=dst[:, f], in_=src)
+                else:
+                    nc.scalar.copy(out=dst[:, f], in_=src)
+            groupeds[unit] = grouped
+
+        def quantise(unit):
+            kind, i = unit
+            nc.vector.quantize_mx(
+                out=codes[kind][:, WORDS * i:WORDS * (i + 1)].bitcast(FP8X4),
+                scales=scales[kind][:, WORDS * i:WORDS * (i + 1)],
+                in_=groupeds[unit][:],
+            )
+
+        for unit in units[0:4]:
+            load(unit)
+        for k in range(2):
+            transpose(units[k], True)
+            load(units[k + 4])
+            quantise(units[k])
+        for n in range(4):
+            spread = psum_m.tile([P, BANK], F32, tag="acc")
+            nc.tensor.matmul(out=spread[:], lhsT=ones[:], rhs=bias_rows[:, BANK * n:BANK * (n + 1)], start=True, stop=True)
+            nc.vector.tensor_copy(out=bias[:, BANK * n:BANK * (n + 1)], in_=spread[:])
+        prepared = 2
+
+        totals = {}
+        means = {}
+
+        def mean_tile(n):
+            if n not in means:
+                means[n] = mean_pool.tile([P, 4, 4, P], F32, name="mean")
+            return means[n]
+
+        def scale(r):
+            n, q = divmod(r, 4)
+            nc.scalar.activation(out=mean_tile(n)[:, :, q, :], in_=totals[r][:], func=COPY, scale=0.25)
+            if r == max(s for s in range(4 * n, 4 * n + 4) if not summed_on_vector(s)):
+                nc.scalar.dma_start(
+                    out=mean_views[n // 2][:, 4 * (n % 2):4 * (n % 2) + 4, :],
+                    in_=means[n][:].rearrange("p h q d -> p h (q d)"),
+                )
+
+        waiting = []
+        scaled = 0
+        for r in range(ROUNDS):
+            n, q = divmod(r, 4)
+            fresh = None
+            if prepared < len(units) and r == first_round(units[prepared - 1]):
+                fresh = units[prepared]
+                transpose(fresh, False)
+                if prepared + 4 < len(units):
+                    load(units[prepared + 4])
+                prepared += 1
+            banks = []
+            for t in range(4):
+                acc = psum_m.tile([P, BANK], F32)
+                for s in range(2):
+                    xo = WORDS * q + 2 * P * t + P * s
+                    wo = WORDS * n + BANK * s
+                    nc.tensor.matmul_mx(
+                        out=acc[:],
+                        lhsT=codes["x"][:, xo:xo + P].bitcast(FP8X4),
+                        lhsT_scale=scales["x"][:, xo:xo + P],
+                        rhs=codes["w"][:, wo:wo + BANK].bitcast(FP8X4),
+                        rhs_scale=scales["w"][:, wo:wo + BANK],
+                        start=(s == 0),
+                        stop=(s == 1),
+                    )
+                banks.append(acc)
+            o = out_pool.tile([P, 4, 4, P], F32)
+            bias_n = bias[:, BANK * n:BANK * (n + 1)].rearrange("p (h d) -> p h d", h=4)
+            if summed_on_vector(r):
+                run = run_pool.tile([P, 4, P], F32)
+            for t in range(4):
+                bank = banks[t][:].rearrange("p (h d) -> p h d", h=4)
+                nc.vector.tensor_tensor(out=o[:, :, t, :], in0=bank, in1=bias_n, op=ADD)
+                if summed_on_vector(r):
+                    nc.vector.scalar_tensor_tensor(
+                        out=(mean_tile(n)[:, :, q, :] if t == 3 else run[:]),
+                        in0=bank,
+                        scalar=0.25,
+                        in1=(bias_n if t == 0 else run[:]),
+                        op0=MULT,
+                        op1=ADD,
+                    )
+                if t == 1 and fresh is not None:
+                    quantise(fresh)
+            nc.sync.dma_start(
+                out=kv_views[n // 2][:, 4 * (n % 2):4 * (n % 2) + 4, BANK * q:BANK * (q + 1)],
+                in_=o[:].rearrange("p h j d -> p h (j d)"),
+            )
+            if not summed_on_vector(r):
+                half = half_pool.tile([P, 4, 2, P], F32)
+                nc.gpsimd.tensor_tensor(out=half[:], in0=o[:, :, 0:2, :], in1=o[:, :, 2:4, :], op=ADD)
+                total = total_pool.tile([P, 4, P], F32)
+                nc.gpsimd.tensor_tensor(out=total[:], in0=half[:, :, 0, :], in1=half[:, :, 1, :], op=ADD)
+                totals[r] = total
+                waiting.append(r)
+            while scaled < len(waiting) and (waiting[scaled] + SCALE_LAG <= r or r == ROUNDS - 1):
+                scale(waiting[scaled])
+                scaled += 1

@@ -35,6 +35,9 @@ def tile_chunkedattention_pb_kernel(tc, hidden_states, wk, bk, wv, bv, out_0, ou
         kind, i = unit
         return i if kind == "x" else 4 * i
 
+    def last_pair(r):
+        return r >= ROUNDS - 2
+
     def summed_on_vector(r):
         return r % 4 == 3 and r > 3
 
@@ -42,7 +45,7 @@ def tile_chunkedattention_pb_kernel(tc, hidden_states, wk, bk, wv, bv, out_0, ou
         const = ctx.enter_context(tc.tile_pool(name="const", bufs=1))
         raw_pool = ctx.enter_context(tc.tile_pool(name="raw_pool", bufs=4))
         grouped_pool = ctx.enter_context(tc.tile_pool(name="grouped_pool", bufs=3))
-        out_pool = ctx.enter_context(tc.tile_pool(name="out_pool", bufs=8))
+        out_pool = ctx.enter_context(tc.tile_pool(name="out_pool", bufs=4))
         half_pool = ctx.enter_context(tc.tile_pool(name="half_pool", bufs=2))
         total_pool = ctx.enter_context(tc.tile_pool(name="total_pool", bufs=SCALE_LAG + 2))
         run_pool = ctx.enter_context(tc.tile_pool(name="run_pool", bufs=2))
@@ -79,8 +82,9 @@ def tile_chunkedattention_pb_kernel(tc, hidden_states, wk, bk, wv, bv, out_0, ou
             else:
                 src = w_views[i // 2][:, i % 2]
             dst = raw[:].rearrange("p (f e) -> p f e", f=4)
-            for f in (0, 2):
-                nc.sync.dma_start(out=dst[:, f:f + 2, :], in_=src[:, f:f + 2, :])
+            step = 2 if unit in units[0:2] else 4
+            for f in range(0, 4, step):
+                nc.sync.dma_start(out=dst[:, f:f + step, :], in_=src[:, f:f + step, :])
             raws[unit] = raw
 
         def transpose(unit, vector_helps):
@@ -170,7 +174,9 @@ def tile_chunkedattention_pb_kernel(tc, hidden_states, wk, bk, wv, bv, out_0, ou
                         stop=(s == 1),
                     )
                 banks.append(acc)
-            o = out_pool.tile([P, 4, 4, P], F32)
+            if q % 2 == 0:
+                pair = out_pool.tile([P, 4, 8, P], F32)
+            o = pair[:, :, 4 * (q % 2):4 * (q % 2) + 4, :]
             bias_n = bias[:, BANK * n:BANK * (n + 1)].rearrange("p (h d) -> p h d", h=4)
             if summed_on_vector(r):
                 run = run_pool.tile([P, 4, P], F32)
@@ -188,10 +194,17 @@ def tile_chunkedattention_pb_kernel(tc, hidden_states, wk, bk, wv, bv, out_0, ou
                     )
                 if t == 1 and fresh is not None:
                     quantise(fresh)
-            nc.sync.dma_start(
-                out=kv_views[n // 2][:, 4 * (n % 2):4 * (n % 2) + 4, BANK * q:BANK * (q + 1)],
-                in_=o[:].rearrange("p h j d -> p h (j d)"),
-            )
+            heads = slice(4 * (n % 2), 4 * (n % 2) + 4)
+            if last_pair(r):
+                nc.sync.dma_start(
+                    out=kv_views[n // 2][:, heads, BANK * q:BANK * (q + 1)],
+                    in_=o.rearrange("p h j d -> p h (j d)"),
+                )
+            elif q % 2 == 1:
+                nc.sync.dma_start(
+                    out=kv_views[n // 2][:, heads, BANK * (q - 1):BANK * (q + 1)],
+                    in_=pair[:].rearrange("p h j d -> p h (j d)"),
+                )
             if not summed_on_vector(r):
                 half = half_pool.tile([P, 4, 2, P], F32)
                 nc.gpsimd.tensor_tensor(out=half[:], in0=o[:, :, 0:2, :], in1=o[:, :, 2:4, :], op=ADD)

@@ -19,6 +19,7 @@ BANK = 512
 UNIT = 4096
 WORDS = UNIT // 4
 ROUNDS = 16
+RAW_BUFS = 6
 SCALE_LAG = 3
 
 
@@ -35,17 +36,14 @@ def tile_chunkedattention_pb_kernel(tc, hidden_states, wk, bk, wv, bv, out_0, ou
         kind, i = unit
         return i if kind == "x" else 4 * i
 
-    def last_pair(r):
-        return r >= ROUNDS - 2
-
     def summed_on_vector(r):
         return r % 4 == 3 and r > 3
 
     with ExitStack() as ctx:
         const = ctx.enter_context(tc.tile_pool(name="const", bufs=1))
-        raw_pool = ctx.enter_context(tc.tile_pool(name="raw_pool", bufs=4))
+        raw_pool = ctx.enter_context(tc.tile_pool(name="raw_pool", bufs=RAW_BUFS))
         grouped_pool = ctx.enter_context(tc.tile_pool(name="grouped_pool", bufs=3))
-        out_pool = ctx.enter_context(tc.tile_pool(name="out_pool", bufs=4))
+        out_pool = ctx.enter_context(tc.tile_pool(name="out_pool", bufs=8))
         half_pool = ctx.enter_context(tc.tile_pool(name="half_pool", bufs=2))
         total_pool = ctx.enter_context(tc.tile_pool(name="total_pool", bufs=SCALE_LAG + 2))
         run_pool = ctx.enter_context(tc.tile_pool(name="run_pool", bufs=2))
@@ -54,14 +52,14 @@ def tile_chunkedattention_pb_kernel(tc, hidden_states, wk, bk, wv, bv, out_0, ou
         psum_m = ctx.enter_context(tc.psum_pool(name="psum_m", bufs=4))
         ctx.enter_context(tc.manual_schedule())
 
+        bias_rows = const.tile([P, P], BF16)
+        nc.vector.memset(bias_rows[:], 0.0)
+        for i, b in enumerate((bk, bv)):
+            nc.sync.dma_start(out=bias_rows[8 * i:8 * i + 8, :], in_=b.rearrange("(h d) -> h d", d=P))
         ident = const.tile([P, P], F32)
         make_identity(nc, ident[:])
-        ones = const.tile([P, P], BF16)
-        nc.vector.memset(ones[:], 1.0)
-        bias_rows = const.tile([P, 4 * BANK], BF16)
-        nc.vector.memset(bias_rows[:], 0.0)
-        nc.scalar.dma_start(out=bias_rows[0:1, 0:2 * BANK], in_=bk.unsqueeze(0))
-        nc.scalar.dma_start(out=bias_rows[0:1, 2 * BANK:4 * BANK], in_=bv.unsqueeze(0))
+        ident_b = const.tile([P, P], BF16)
+        nc.vector.tensor_copy(out=ident_b[:], in_=ident[:])
         bias = const.tile([P, 4 * BANK], F32)
         codes = {
             "x": const.tile([P, 4 * WORDS], U32, align_bytes=64, name="x_codes"),
@@ -118,16 +116,29 @@ def tile_chunkedattention_pb_kernel(tc, hidden_states, wk, bk, wv, bv, out_0, ou
                 in_=groupeds[unit][:],
             )
 
-        for unit in units[0:4]:
+        def spread_bias(n):
+            spread = psum_m.tile([P, BANK], F32, tag="acc")
+            for h in range(4):
+                r = 4 * n + h
+                nc.tensor.matmul(
+                    out=spread[:, P * h:P * (h + 1)],
+                    lhsT=ident_b[:, r:r + 1].to_broadcast([P, P]),
+                    rhs=bias_rows[:],
+                    start=True,
+                    stop=True,
+                )
+            nc.scalar.copy(out=bias[:, BANK * n:BANK * (n + 1)], in_=spread[:])
+
+        for unit in units[0:RAW_BUFS]:
             load(unit)
         for k in range(2):
             transpose(units[k], True)
-            load(units[k + 4])
+            load(units[k + RAW_BUFS])
+            if k == 0:
+                spread_bias(0)
             quantise(units[k])
-        for n in range(4):
-            spread = psum_m.tile([P, BANK], F32, tag="acc")
-            nc.tensor.matmul(out=spread[:], lhsT=ones[:], rhs=bias_rows[:, BANK * n:BANK * (n + 1)], start=True, stop=True)
-            nc.vector.tensor_copy(out=bias[:, BANK * n:BANK * (n + 1)], in_=spread[:])
+        for n in range(1, 4):
+            spread_bias(n)
         prepared = 2
 
         totals = {}
@@ -155,8 +166,6 @@ def tile_chunkedattention_pb_kernel(tc, hidden_states, wk, bk, wv, bv, out_0, ou
             if prepared < len(units) and r == first_round(units[prepared - 1]):
                 fresh = units[prepared]
                 transpose(fresh, False)
-                if prepared + 4 < len(units):
-                    load(units[prepared + 4])
                 prepared += 1
             banks = []
             for t in range(4):
@@ -174,9 +183,7 @@ def tile_chunkedattention_pb_kernel(tc, hidden_states, wk, bk, wv, bv, out_0, ou
                         stop=(s == 1),
                     )
                 banks.append(acc)
-            if q % 2 == 0:
-                pair = out_pool.tile([P, 4, 8, P], F32)
-            o = pair[:, :, 4 * (q % 2):4 * (q % 2) + 4, :]
+            o = out_pool.tile([P, 4, 4, P], F32)
             bias_n = bias[:, BANK * n:BANK * (n + 1)].rearrange("p (h d) -> p h d", h=4)
             if summed_on_vector(r):
                 run = run_pool.tile([P, 4, P], F32)
@@ -192,19 +199,12 @@ def tile_chunkedattention_pb_kernel(tc, hidden_states, wk, bk, wv, bv, out_0, ou
                         op0=MULT,
                         op1=ADD,
                     )
-                if t == 1 and fresh is not None:
-                    quantise(fresh)
-            heads = slice(4 * (n % 2), 4 * (n % 2) + 4)
-            if last_pair(r):
-                nc.sync.dma_start(
-                    out=kv_views[n // 2][:, heads, BANK * q:BANK * (q + 1)],
-                    in_=o.rearrange("p h j d -> p h (j d)"),
-                )
-            elif q % 2 == 1:
-                nc.sync.dma_start(
-                    out=kv_views[n // 2][:, heads, BANK * (q - 1):BANK * (q + 1)],
-                    in_=pair[:].rearrange("p h j d -> p h (j d)"),
-                )
+            if fresh is not None:
+                quantise(fresh)
+            nc.sync.dma_start(
+                out=kv_views[n // 2][:, 4 * (n % 2):4 * (n % 2) + 4, BANK * q:BANK * (q + 1)],
+                in_=o[:].rearrange("p h j d -> p h (j d)"),
+            )
             if not summed_on_vector(r):
                 half = half_pool.tile([P, 4, 2, P], F32)
                 nc.gpsimd.tensor_tensor(out=half[:], in0=o[:, :, 0:2, :], in1=o[:, :, 2:4, :], op=ADD)

@@ -37,7 +37,7 @@ def tile_chunkedattention_pb_kernel(tc, hidden_states, wk, bk, wv, bv, out_0, ou
         return i if kind == "x" else 4 * i
 
     def summed_on_vector(r):
-        return r % 4 == 3 and r > 3
+        return r % 4 == 3 or r == 13
 
     with ExitStack() as ctx:
         const = ctx.enter_context(tc.tile_pool(name="const", bufs=1))
@@ -199,8 +199,8 @@ def tile_chunkedattention_pb_kernel(tc, hidden_states, wk, bk, wv, bv, out_0, ou
                         op0=MULT,
                         op1=ADD,
                     )
-            if fresh is not None:
-                quantise(fresh)
+                if t == 1 and fresh is not None:
+                    quantise(fresh)
             nc.sync.dma_start(
                 out=kv_views[n // 2][:, 4 * (n % 2):4 * (n % 2) + 4, BANK * q:BANK * (q + 1)],
                 in_=o[:].rearrange("p h j d -> p h (j d)"),

@@ -19,8 +19,8 @@ BANK = 512
 UNIT = 4096
 WORDS = UNIT // 4
 ROUNDS = 16
-RAW_BUFS = 6
-SCALE_LAG = 3
+RAW_BUFS = 4
+SCALE_LAG = 4
 
 
 def tile_chunkedattention_pb_kernel(tc, hidden_states, wk, bk, wv, bv, out_0, out_1, out_2, out_3):
@@ -30,24 +30,26 @@ def tile_chunkedattention_pb_kernel(tc, hidden_states, wk, bk, wv, bv, out_0, ou
     kv_views = [o.rearrange("b h (p q) t d -> p (b h) (q t d)", p=P, q=4) for o in (out_0, out_1)]
     mean_views = [o.rearrange("b h (p q) d -> p (b h) (q d)", p=P, q=4) for o in (out_2, out_3)]
 
-    units = [("w", 0), ("x", 0), ("x", 1), ("x", 2), ("x", 3), ("w", 1), ("w", 2), ("w", 3)]
-
-    def first_round(unit):
-        kind, i = unit
-        return i if kind == "x" else 4 * i
+    units = [("w", 0), ("x", 0), ("x", 1), ("w", 1), ("x", 2), ("x", 3), ("w", 2), ("w", 3)]
+    rounds = [(0, 0), (0, 1), (1, 0), (1, 1), (0, 2), (1, 2), (0, 3), (1, 3)]
+    rounds += [(n, q) for n in (2, 3) for q in range(4)]
+    prepared_in = {unit: r for r, unit in enumerate(units[2:6])}
+    prepared_in.update({("w", n): 4 * n - 1 for n in (2, 3)})
+    ordered_first = units[4:8]
 
     def summed_on_vector(r):
-        return r % 4 == 3 or r == 13
+        return r in (6, 10, 14, 15)
 
     with ExitStack() as ctx:
         const = ctx.enter_context(tc.tile_pool(name="const", bufs=1))
         raw_pool = ctx.enter_context(tc.tile_pool(name="raw_pool", bufs=RAW_BUFS))
+        ordered_pool = ctx.enter_context(tc.tile_pool(name="ordered_pool", bufs=2))
         grouped_pool = ctx.enter_context(tc.tile_pool(name="grouped_pool", bufs=3))
         out_pool = ctx.enter_context(tc.tile_pool(name="out_pool", bufs=8))
         half_pool = ctx.enter_context(tc.tile_pool(name="half_pool", bufs=2))
         total_pool = ctx.enter_context(tc.tile_pool(name="total_pool", bufs=SCALE_LAG + 2))
         run_pool = ctx.enter_context(tc.tile_pool(name="run_pool", bufs=2))
-        mean_pool = ctx.enter_context(tc.tile_pool(name="mean_pool", bufs=2))
+        mean_pool = ctx.enter_context(tc.tile_pool(name="mean_pool", bufs=3))
         psum_t = ctx.enter_context(tc.psum_pool(name="psum_t", bufs=4))
         psum_m = ctx.enter_context(tc.psum_pool(name="psum_m", bufs=4))
         ctx.enter_context(tc.manual_schedule())
@@ -70,6 +72,7 @@ def tile_chunkedattention_pb_kernel(tc, hidden_states, wk, bk, wv, bv, out_0, ou
             "w": const.tile([P, 4 * WORDS], U8, align_bytes=64, name="w_scales"),
         }
         raws = {}
+        ordereds = {}
         groupeds = {}
 
         def load(unit):
@@ -85,9 +88,25 @@ def tile_chunkedattention_pb_kernel(tc, hidden_states, wk, bk, wv, bv, out_0, ou
                 nc.sync.dma_start(out=dst[:, f:f + step, :], in_=src[:, f:f + step, :])
             raws[unit] = raw
 
+        def load_behind(unit):
+            k = units.index(unit) + RAW_BUFS
+            if k < len(units):
+                load(units[k])
+
+        def order(unit):
+            ordered = ordered_pool.tile([P, UNIT], BF16)
+            for half in range(2):
+                words = slice(2 * BANK * half, 2 * BANK * (half + 1))
+                nc.scalar.copy(
+                    out=ordered[:].bitcast(F32)[:, words].rearrange("p (b u c) -> p b u c", b=4, u=2, c=P),
+                    in_=raws[unit][:].bitcast(F32)[:, words].rearrange("p (b c u) -> p b u c", b=4, u=2, c=P),
+                )
+            ordereds[unit] = ordered
+            load_behind(unit)
+
         def transpose(unit, vector_helps):
             kind = unit[0]
-            raw_words = raws[unit][:].bitcast(F32)
+            raw_words = (ordereds if unit in ordereds else raws)[unit][:].bitcast(F32)
             grouped = grouped_pool.tile([P, UNIT], BF16, align_bytes=64)
             grouped_words = grouped[:].bitcast(F32)
             if kind == "x":
@@ -97,16 +116,21 @@ def tile_chunkedattention_pb_kernel(tc, hidden_states, wk, bk, wv, bv, out_0, ou
             for f in range(4):
                 turned = psum_t.tile([P, BANK], F32)
                 for a in range(4):
-                    lo = BANK * f + 2 * P * (a // 2)
-                    nc.tensor.transpose(
-                        turned[:, P * a:P * (a + 1)], raw_words[:, lo + a % 2:lo + 2 * P:2], ident[:]
-                    )
+                    if unit in ordereds:
+                        lo = BANK * f + P * a
+                        block = raw_words[:, lo:lo + P]
+                    else:
+                        lo = BANK * f + 2 * P * (a // 2)
+                        block = raw_words[:, lo + a % 2:lo + 2 * P:2]
+                    nc.tensor.transpose(turned[:, P * a:P * (a + 1)], block, ident[:])
                 src = turned[:].rearrange("p (s u c) -> p s c u", s=2, u=2, c=P)
                 if vector_helps and f % 2 == 1:
                     nc.vector.tensor_copy(out=dst[:, f], in_=src)
                 else:
                     nc.scalar.copy(out=dst[:, f], in_=src)
             groupeds[unit] = grouped
+            if unit not in ordereds:
+                load_behind(unit)
 
         def quantise(unit):
             kind, i = unit
@@ -133,13 +157,11 @@ def tile_chunkedattention_pb_kernel(tc, hidden_states, wk, bk, wv, bv, out_0, ou
             load(unit)
         for k in range(2):
             transpose(units[k], True)
-            load(units[k + RAW_BUFS])
             if k == 0:
                 spread_bias(0)
             quantise(units[k])
         for n in range(1, 4):
             spread_bias(n)
-        prepared = 2
 
         totals = {}
         means = {}
@@ -150,9 +172,9 @@ def tile_chunkedattention_pb_kernel(tc, hidden_states, wk, bk, wv, bv, out_0, ou
             return means[n]
 
         def scale(r):
-            n, q = divmod(r, 4)
+            n, q = rounds[r]
             nc.scalar.activation(out=mean_tile(n)[:, :, q, :], in_=totals[r][:], func=COPY, scale=0.25)
-            if r == max(s for s in range(4 * n, 4 * n + 4) if not summed_on_vector(s)):
+            if r == max(s for s in range(ROUNDS) if rounds[s][0] == n and not summed_on_vector(s)):
                 nc.scalar.dma_start(
                     out=mean_views[n // 2][:, 4 * (n % 2):4 * (n % 2) + 4, :],
                     in_=means[n][:].rearrange("p h q d -> p h (q d)"),
@@ -161,12 +183,15 @@ def tile_chunkedattention_pb_kernel(tc, hidden_states, wk, bk, wv, bv, out_0, ou
         waiting = []
         scaled = 0
         for r in range(ROUNDS):
-            n, q = divmod(r, 4)
+            n, q = rounds[r]
+            for unit in ordered_first:
+                if r == prepared_in[unit] - 1:
+                    order(unit)
             fresh = None
-            if prepared < len(units) and r == first_round(units[prepared - 1]):
-                fresh = units[prepared]
-                transpose(fresh, False)
-                prepared += 1
+            for unit in units[2:]:
+                if r == prepared_in[unit]:
+                    fresh = unit
+                    transpose(unit, False)
             banks = []
             for t in range(4):
                 acc = psum_m.tile([P, BANK], F32)

@@ -19,7 +19,7 @@ BANK = 512
 UNIT = 4096
 WORDS = UNIT // 4
 ROUNDS = 16
-RAW_BUFS = 4
+RAW_BUFS = 6
 SCALE_LAG = 4
 
 
@@ -35,15 +35,13 @@ def tile_chunkedattention_pb_kernel(tc, hidden_states, wk, bk, wv, bv, out_0, ou
     rounds += [(n, q) for n in (2, 3) for q in range(4)]
     prepared_in = {unit: r for r, unit in enumerate(units[2:6])}
     prepared_in.update({("w", n): 4 * n - 1 for n in (2, 3)})
-    ordered_first = units[4:8]
 
     def summed_on_vector(r):
-        return r in (6, 10, 14, 15)
+        return r in (6, 10, 13, 15)
 
     with ExitStack() as ctx:
         const = ctx.enter_context(tc.tile_pool(name="const", bufs=1))
         raw_pool = ctx.enter_context(tc.tile_pool(name="raw_pool", bufs=RAW_BUFS))
-        ordered_pool = ctx.enter_context(tc.tile_pool(name="ordered_pool", bufs=2))
         grouped_pool = ctx.enter_context(tc.tile_pool(name="grouped_pool", bufs=3))
         out_pool = ctx.enter_context(tc.tile_pool(name="out_pool", bufs=8))
         half_pool = ctx.enter_context(tc.tile_pool(name="half_pool", bufs=2))
@@ -72,7 +70,6 @@ def tile_chunkedattention_pb_kernel(tc, hidden_states, wk, bk, wv, bv, out_0, ou
             "w": const.tile([P, 4 * WORDS], U8, align_bytes=64, name="w_scales"),
         }
         raws = {}
-        ordereds = {}
         groupeds = {}
 
         def load(unit):
@@ -93,20 +90,9 @@ def tile_chunkedattention_pb_kernel(tc, hidden_states, wk, bk, wv, bv, out_0, ou
             if k < len(units):
                 load(units[k])
 
-        def order(unit):
-            ordered = ordered_pool.tile([P, UNIT], BF16)
-            for half in range(2):
-                words = slice(2 * BANK * half, 2 * BANK * (half + 1))
-                nc.scalar.copy(
-                    out=ordered[:].bitcast(F32)[:, words].rearrange("p (b u c) -> p b u c", b=4, u=2, c=P),
-                    in_=raws[unit][:].bitcast(F32)[:, words].rearrange("p (b c u) -> p b u c", b=4, u=2, c=P),
-                )
-            ordereds[unit] = ordered
-            load_behind(unit)
-
         def transpose(unit, vector_helps):
             kind = unit[0]
-            raw_words = (ordereds if unit in ordereds else raws)[unit][:].bitcast(F32)
+            raw_words = raws[unit][:].bitcast(F32)
             grouped = grouped_pool.tile([P, UNIT], BF16, align_bytes=64)
             grouped_words = grouped[:].bitcast(F32)
             if kind == "x":
@@ -116,21 +102,17 @@ def tile_chunkedattention_pb_kernel(tc, hidden_states, wk, bk, wv, bv, out_0, ou
             for f in range(4):
                 turned = psum_t.tile([P, BANK], F32)
                 for a in range(4):
-                    if unit in ordereds:
-                        lo = BANK * f + P * a
-                        block = raw_words[:, lo:lo + P]
-                    else:
-                        lo = BANK * f + 2 * P * (a // 2)
-                        block = raw_words[:, lo + a % 2:lo + 2 * P:2]
-                    nc.tensor.transpose(turned[:, P * a:P * (a + 1)], block, ident[:])
+                    lo = BANK * f + 2 * P * (a // 2)
+                    nc.tensor.transpose(
+                        turned[:, P * a:P * (a + 1)], raw_words[:, lo + a % 2:lo + 2 * P:2], ident[:]
+                    )
                 src = turned[:].rearrange("p (s u c) -> p s c u", s=2, u=2, c=P)
                 if vector_helps and f % 2 == 1:
                     nc.vector.tensor_copy(out=dst[:, f], in_=src)
                 else:
                     nc.scalar.copy(out=dst[:, f], in_=src)
             groupeds[unit] = grouped
-            if unit not in ordereds:
-                load_behind(unit)
+            load_behind(unit)
 
         def quantise(unit):
             kind, i = unit
@@ -184,9 +166,6 @@ def tile_chunkedattention_pb_kernel(tc, hidden_states, wk, bk, wv, bv, out_0, ou
         scaled = 0
         for r in range(ROUNDS):
             n, q = rounds[r]
-            for unit in ordered_first:
-                if r == prepared_in[unit] - 1:
-                    order(unit)
             fresh = None
             for unit in units[2:]:
                 if r == prepared_in[unit]:

@@ -54,8 +54,6 @@ def tile_chunkedattention_pb_kernel(tc, hidden_states, wk, bk, wv, bv, out_0, ou
 
         bias_rows = const.tile([P, P], BF16)
         nc.vector.memset(bias_rows[:], 0.0)
-        for i, b in enumerate((bk, bv)):
-            nc.sync.dma_start(out=bias_rows[8 * i:8 * i + 8, :], in_=b.rearrange("(h d) -> h d", d=P))
         ident = const.tile([P, P], F32)
         make_identity(nc, ident[:])
         ident_b = const.tile([P, P], BF16)
@@ -80,7 +78,7 @@ def tile_chunkedattention_pb_kernel(tc, hidden_states, wk, bk, wv, bv, out_0, ou
             else:
                 src = w_views[i // 2][:, i % 2]
             dst = raw[:].rearrange("p (f e) -> p f e", f=4)
-            step = 2 if unit in units[0:2] else 4
+            step = 2 if unit in units[0:3] else 4
             for f in range(0, 4, step):
                 nc.sync.dma_start(out=dst[:, f:f + step, :], in_=src[:, f:f + step, :])
             raws[unit] = raw
@@ -90,16 +88,17 @@ def tile_chunkedattention_pb_kernel(tc, hidden_states, wk, bk, wv, bv, out_0, ou
             if k < len(units):
                 load(units[k])
 
-        def transpose(unit, vector_helps):
+        def transpose(unit, fs, vector_helps):
             kind = unit[0]
             raw_words = raws[unit][:].bitcast(F32)
-            grouped = grouped_pool.tile([P, UNIT], BF16, align_bytes=64)
-            grouped_words = grouped[:].bitcast(F32)
+            if unit not in groupeds:
+                groupeds[unit] = grouped_pool.tile([P, UNIT], BF16, align_bytes=64, name="grouped")
+            grouped_words = groupeds[unit][:].bitcast(F32)
             if kind == "x":
                 dst = grouped_words.rearrange("p (f s c u) -> p f s c u", f=4, s=2, c=P, u=2)
             else:
                 dst = grouped_words.rearrange("p (s f c u) -> p f s c u", s=2, f=4, c=P, u=2)
-            for f in range(4):
+            for f in fs:
                 turned = psum_t.tile([P, BANK], F32)
                 for a in range(4):
                     lo = BANK * f + 2 * P * (a // 2)
@@ -111,15 +110,17 @@ def tile_chunkedattention_pb_kernel(tc, hidden_states, wk, bk, wv, bv, out_0, ou
                     nc.vector.tensor_copy(out=dst[:, f], in_=src)
                 else:
                     nc.scalar.copy(out=dst[:, f], in_=src)
-            groupeds[unit] = grouped
-            load_behind(unit)
+            if fs[-1] == 3:
+                load_behind(unit)
 
-        def quantise(unit):
+        def quantise(unit, part=0, parts=1):
             kind, i = unit
+            size = WORDS // parts
+            lo = WORDS * i + size * part
             nc.vector.quantize_mx(
-                out=codes[kind][:, WORDS * i:WORDS * (i + 1)].bitcast(FP8X4),
-                scales=scales[kind][:, WORDS * i:WORDS * (i + 1)],
-                in_=groupeds[unit][:],
+                out=codes[kind][:, lo:lo + size].bitcast(FP8X4),
+                scales=scales[kind][:, lo:lo + size],
+                in_=groupeds[unit][:, 4 * size * part:4 * size * (part + 1)],
             )
 
         def spread_bias(n):
@@ -137,13 +138,16 @@ def tile_chunkedattention_pb_kernel(tc, hidden_states, wk, bk, wv, bv, out_0, ou
 
         for unit in units[0:RAW_BUFS]:
             load(unit)
-        for k in range(2):
-            transpose(units[k], True)
-            if k == 0:
-                spread_bias(0)
-            quantise(units[k])
-        for n in range(1, 4):
-            spread_bias(n)
+            if unit == units[0]:
+                for i, b in enumerate((bk, bv)):
+                    nc.sync.dma_start(out=bias_rows[8 * i:8 * i + 8, :], in_=b.rearrange("(h d) -> h d", d=P))
+        transpose(units[0], range(4), True)
+        spread_bias(0)
+        quantise(units[0])
+        for half in range(2):
+            transpose(units[1], (2 * half, 2 * half + 1), True)
+            quantise(units[1], half, 2)
+        spread_bias(1)
 
         totals = {}
         means = {}
@@ -156,10 +160,12 @@ def tile_chunkedattention_pb_kernel(tc, hidden_states, wk, bk, wv, bv, out_0, ou
         def scale(r):
             n, q = rounds[r]
             nc.scalar.activation(out=mean_tile(n)[:, :, q, :], in_=totals[r][:], func=COPY, scale=0.25)
-            if r == max(s for s in range(ROUNDS) if rounds[s][0] == n and not summed_on_vector(s)):
+            first, size = (q // 2 * 2, 2) if n == 3 else (0, 4)
+            qs = range(first, first + size)
+            if r == max(s for s in range(ROUNDS) if rounds[s][0] == n and rounds[s][1] in qs and not summed_on_vector(s)):
                 nc.scalar.dma_start(
-                    out=mean_views[n // 2][:, 4 * (n % 2):4 * (n % 2) + 4, :],
-                    in_=means[n][:].rearrange("p h q d -> p h (q d)"),
+                    out=mean_views[n // 2][:, 4 * (n % 2):4 * (n % 2) + 4, P * first:P * (first + size)],
+                    in_=means[n][:, :, first:first + size, :].rearrange("p h q d -> p h (q d)"),
                 )
 
         waiting = []
@@ -170,9 +176,12 @@ def tile_chunkedattention_pb_kernel(tc, hidden_states, wk, bk, wv, bv, out_0, ou
             for unit in units[2:]:
                 if r == prepared_in[unit]:
                     fresh = unit
-                    transpose(unit, False)
+            if r in (5, 9):
+                spread_bias(r // 4 + 1)
             banks = []
             for t in range(4):
+                if fresh is not None and t == 0:
+                    transpose(fresh, range(4), False)
                 acc = psum_m.tile([P, BANK], F32)
                 for s in range(2):
                     xo = WORDS * q + 2 * P * t + P * s
@@ -186,23 +195,31 @@ def tile_chunkedattention_pb_kernel(tc, hidden_states, wk, bk, wv, bv, out_0, ou
                         start=(s == 0),
                         stop=(s == 1),
                     )
-                banks.append(acc)
+                banks.append(acc[:].rearrange("p (h d) -> p h d", h=4))
             o = out_pool.tile([P, 4, 4, P], F32)
             bias_n = bias[:, BANK * n:BANK * (n + 1)].rearrange("p (h d) -> p h d", h=4)
             if summed_on_vector(r):
                 run = run_pool.tile([P, 4, P], F32)
-            for t in range(4):
-                bank = banks[t][:].rearrange("p (h d) -> p h d", h=4)
-                nc.vector.tensor_tensor(out=o[:, :, t, :], in0=bank, in1=bias_n, op=ADD)
-                if summed_on_vector(r):
-                    nc.vector.scalar_tensor_tensor(
-                        out=(mean_tile(n)[:, :, q, :] if t == 3 else run[:]),
-                        in0=bank,
-                        scalar=0.25,
-                        in1=(bias_n if t == 0 else run[:]),
-                        op0=MULT,
-                        op1=ADD,
-                    )
+
+            def add_bias(t):
+                nc.vector.tensor_tensor(out=o[:, :, t, :], in0=banks[t], in1=bias_n, op=ADD)
+
+            def add_to_mean(t):
+                nc.vector.scalar_tensor_tensor(
+                    out=(mean_tile(n)[:, :, q, :] if t == 3 else run[:]),
+                    in0=banks[t],
+                    scalar=0.25,
+                    in1=(bias_n if t == 0 else run[:]),
+                    op0=MULT,
+                    op1=ADD,
+                )
+
+            behind = 1 if r == ROUNDS - 1 else 0
+            for t in range(4 + behind):
+                if t < 4:
+                    add_bias(t)
+                if summed_on_vector(r) and t >= behind:
+                    add_to_mean(t - behind)
                 if t == 1 and fresh is not None:
                     quantise(fresh)
             nc.sync.dma_start(

@@ -20,13 +20,13 @@ UNIT = 4096
 WORDS = UNIT // 4
 ROUNDS = 16
 RAW_BUFS = 6
-SCALE_LAG = 4
+SCALE_LAG = 3
 
 
 def tile_chunkedattention_pb_kernel(tc, hidden_states, wk, bk, wv, bv, out_0, out_1, out_2, out_3):
     nc = tc.nc
     x_view = hidden_states.flatten_outer_dims().rearrange("(p q t) e -> p q (t e)", p=P, q=4, t=4)
-    w_views = [w.rearrange("(n f p) e -> p n f e", n=2, f=4, p=P) for w in (wk, wv)]
+    w_views = [w.rearrange("(n j p f) e -> p n j (f e)", n=2, j=2, p=P, f=2) for w in (wk, wv)]
     kv_views = [o.rearrange("b h (p q) t d -> p (b h) (q t d)", p=P, q=4) for o in (out_0, out_1)]
     mean_views = [o.rearrange("b h (p q) d -> p (b h) (q d)", p=P, q=4) for o in (out_2, out_3)]
 
@@ -74,13 +74,13 @@ def tile_chunkedattention_pb_kernel(tc, hidden_states, wk, bk, wv, bv, out_0, ou
             kind, i = unit
             raw = raw_pool.tile([P, UNIT], BF16)
             if kind == "x":
-                src = x_view[:, i, :].rearrange("p (f e) -> p f e", f=4)
+                src = x_view[:, i, :].rearrange("p (j e) -> p j e", j=2)
             else:
                 src = w_views[i // 2][:, i % 2]
-            dst = raw[:].rearrange("p (f e) -> p f e", f=4)
-            step = 2 if unit in units[0:3] else 4
-            for f in range(0, 4, step):
-                nc.sync.dma_start(out=dst[:, f:f + step, :], in_=src[:, f:f + step, :])
+            dst = raw[:].rearrange("p (j e) -> p j e", j=2)
+            step = 1 if unit in units[0:3] else 2
+            for j in range(0, 2, step):
+                nc.sync.dma_start(out=dst[:, j:j + step, :], in_=src[:, j:j + step, :])
             raws[unit] = raw
 
         def load_behind(unit):
@@ -88,29 +88,38 @@ def tile_chunkedattention_pb_kernel(tc, hidden_states, wk, bk, wv, bv, out_0, ou
             if k < len(units):
                 load(units[k])
 
-        def transpose(unit, fs, vector_helps):
+        def transpose(unit, banks_of_unit, vector_helps):
             kind = unit[0]
             raw_words = raws[unit][:].bitcast(F32)
             if unit not in groupeds:
                 groupeds[unit] = grouped_pool.tile([P, UNIT], BF16, align_bytes=64, name="grouped")
             grouped_words = groupeds[unit][:].bitcast(F32)
-            if kind == "x":
-                dst = grouped_words.rearrange("p (f s c u) -> p f s c u", f=4, s=2, c=P, u=2)
-            else:
-                dst = grouped_words.rearrange("p (s f c u) -> p f s c u", s=2, f=4, c=P, u=2)
-            for f in fs:
+            for b in banks_of_unit:
+                if kind == "x":
+                    starts = [BANK * b + 2 * P * s for s in range(2)]
+                    lo = BANK * b
+                else:
+                    j, s = divmod(b, 2)
+                    starts = [BANK * (2 * j + f) + 2 * P * s for f in range(2)]
+                    lo = BANK * (2 * s + j)
                 turned = psum_t.tile([P, BANK], F32)
                 for a in range(4):
-                    lo = BANK * f + 2 * P * (a // 2)
+                    start = starts[a // 2]
                     nc.tensor.transpose(
-                        turned[:, P * a:P * (a + 1)], raw_words[:, lo + a % 2:lo + 2 * P:2], ident[:]
+                        turned[:, P * a:P * (a + 1)], raw_words[:, start + a % 2:start + 2 * P:2], ident[:]
                     )
-                src = turned[:].rearrange("p (s u c) -> p s c u", s=2, u=2, c=P)
-                if vector_helps and f % 2 == 1:
-                    nc.vector.tensor_copy(out=dst[:, f], in_=src)
+                dst = grouped_words[:, lo:lo + BANK]
+                if kind == "x":
+                    src = turned[:].rearrange("p (s u c) -> p s c u", s=2, u=2, c=P)
+                    dst = dst.rearrange("p (s c u) -> p s c u", s=2, c=P, u=2)
                 else:
-                    nc.scalar.copy(out=dst[:, f], in_=src)
-            if fs[-1] == 3:
+                    src = turned[:].rearrange("p (f u c) -> p c f u", f=2, u=2, c=P)
+                    dst = dst.rearrange("p (c f u) -> p c f u", c=P, f=2, u=2)
+                if vector_helps and b % 2 == 1:
+                    nc.vector.tensor_copy(out=dst, in_=src)
+                else:
+                    nc.scalar.copy(out=dst, in_=src)
+            if banks_of_unit[-1] == 3:
                 load_behind(unit)
 
         def quantise(unit, part=0, parts=1):
@@ -160,12 +169,10 @@ def tile_chunkedattention_pb_kernel(tc, hidden_states, wk, bk, wv, bv, out_0, ou
         def scale(r):
             n, q = rounds[r]
             nc.scalar.activation(out=mean_tile(n)[:, :, q, :], in_=totals[r][:], func=COPY, scale=0.25)
-            first, size = (q // 2 * 2, 2) if n == 3 else (0, 4)
-            qs = range(first, first + size)
-            if r == max(s for s in range(ROUNDS) if rounds[s][0] == n and rounds[s][1] in qs and not summed_on_vector(s)):
+            if r == max(s for s in range(ROUNDS) if rounds[s][0] == n and not summed_on_vector(s)):
                 nc.scalar.dma_start(
-                    out=mean_views[n // 2][:, 4 * (n % 2):4 * (n % 2) + 4, P * first:P * (first + size)],
-                    in_=means[n][:, :, first:first + size, :].rearrange("p h q d -> p h (q d)"),
+                    out=mean_views[n // 2][:, 4 * (n % 2):4 * (n % 2) + 4, :],
+                    in_=means[n][:].rearrange("p h q d -> p h (q d)"),
                 )
 
         waiting = []

from contextlib import ExitStack

import concourse.mybir as mybir
from concourse.masks import make_identity

F32 = mybir.dt.float32
BF16 = mybir.dt.bfloat16
U32 = mybir.dt.uint32
U8 = mybir.dt.uint8
FP8X4 = mybir.dt.float8_e4m3fn_x4
ADD = mybir.AluOpType.add
MULT = mybir.AluOpType.mult
COPY = mybir.ActivationFunctionType.Copy

FLOPS = 2 * 2048 * 1024 * 2048

P = 128
BANK = 512
UNIT = 4096
WORDS = UNIT // 4
ROUNDS = 16
RAW_BUFS = 6
SCALE_LAG = 3


def tile_chunkedattention_pb_kernel(tc, hidden_states, wk, bk, wv, bv, out_0, out_1, out_2, out_3):
    nc = tc.nc
    x_view = hidden_states.flatten_outer_dims().rearrange("(p q t) e -> p q (t e)", p=P, q=4, t=4)
    w_views = [w.rearrange("(n j p f) e -> p n j (f e)", n=2, j=2, p=P, f=2) for w in (wk, wv)]
    kv_views = [o.rearrange("b h (p q) t d -> p (b h) (q t d)", p=P, q=4) for o in (out_0, out_1)]
    mean_views = [o.rearrange("b h (p q) d -> p (b h) (q d)", p=P, q=4) for o in (out_2, out_3)]

    units = [("w", 0), ("x", 0), ("x", 1), ("w", 1), ("x", 2), ("x", 3), ("w", 2), ("w", 3)]
    rounds = [(0, 0), (0, 1), (1, 0), (1, 1), (0, 2), (1, 2), (0, 3), (1, 3)]
    rounds += [(n, q) for n in (2, 3) for q in range(4)]
    prepared_in = {unit: r for r, unit in enumerate(units[2:6])}
    prepared_in.update({("w", n): 4 * n - 1 for n in (2, 3)})

    def summed_on_vector(r):
        return r in (6, 10, 13, 15)

    with ExitStack() as ctx:
        const = ctx.enter_context(tc.tile_pool(name="const", bufs=1))
        raw_pool = ctx.enter_context(tc.tile_pool(name="raw_pool", bufs=RAW_BUFS))
        grouped_pool = ctx.enter_context(tc.tile_pool(name="grouped_pool", bufs=3))
        out_pool = ctx.enter_context(tc.tile_pool(name="out_pool", bufs=8))
        half_pool = ctx.enter_context(tc.tile_pool(name="half_pool", bufs=2))
        total_pool = ctx.enter_context(tc.tile_pool(name="total_pool", bufs=SCALE_LAG + 2))
        run_pool = ctx.enter_context(tc.tile_pool(name="run_pool", bufs=2))
        mean_pool = ctx.enter_context(tc.tile_pool(name="mean_pool", bufs=3))
        psum_t = ctx.enter_context(tc.psum_pool(name="psum_t", bufs=4))
        psum_m = ctx.enter_context(tc.psum_pool(name="psum_m", bufs=4))
        ctx.enter_context(tc.manual_schedule())

        bias_rows = const.tile([P, P], BF16)
        nc.vector.memset(bias_rows[:], 0.0)
        ident = const.tile([P, P], F32)
        make_identity(nc, ident[:])
        ident_b = const.tile([P, P], BF16)
        nc.vector.tensor_copy(out=ident_b[:], in_=ident[:])
        bias = const.tile([P, 4 * BANK], F32)
        codes = {
            "x": const.tile([P, 4 * WORDS], U32, align_bytes=64, name="x_codes"),
            "w": const.tile([P, 4 * WORDS], U32, align_bytes=64, name="w_codes"),
        }
        scales = {
            "x": const.tile([P, 4 * WORDS], U8, align_bytes=64, name="x_scales"),
            "w": const.tile([P, 4 * WORDS], U8, align_bytes=64, name="w_scales"),
        }
        raws = {}
        groupeds = {}

        def load(unit):
            kind, i = unit
            raw = raw_pool.tile([P, UNIT], BF16)
            if kind == "x":
                src = x_view[:, i, :].rearrange("p (j e) -> p j e", j=2)
            else:
                src = w_views[i // 2][:, i % 2]
            dst = raw[:].rearrange("p (j e) -> p j e", j=2)
            step = 1 if unit in units[0:3] else 2
            for j in range(0, 2, step):
                nc.sync.dma_start(out=dst[:, j:j + step, :], in_=src[:, j:j + step, :])
            raws[unit] = raw

        def load_behind(unit):
            k = units.index(unit) + RAW_BUFS
            if k < len(units):
                load(units[k])

        def transpose(unit, banks_of_unit, vector_helps):
            kind = unit[0]
            raw_words = raws[unit][:].bitcast(F32)
            if unit not in groupeds:
                groupeds[unit] = grouped_pool.tile([P, UNIT], BF16, align_bytes=64, name="grouped")
            grouped_words = groupeds[unit][:].bitcast(F32)
            for b in banks_of_unit:
                if kind == "x":
                    starts = [BANK * b + 2 * P * s for s in range(2)]
                    lo = BANK * b
                else:
                    j, s = divmod(b, 2)
                    starts = [BANK * (2 * j + f) + 2 * P * s for f in range(2)]
                    lo = BANK * (2 * s + j)
                turned = psum_t.tile([P, BANK], F32)
                for a in range(4):
                    start = starts[a // 2]
                    nc.tensor.transpose(
                        turned[:, P * a:P * (a + 1)], raw_words[:, start + a % 2:start + 2 * P:2], ident[:]
                    )
                dst = grouped_words[:, lo:lo + BANK]
                if kind == "x":
                    src = turned[:].rearrange("p (s u c) -> p s c u", s=2, u=2, c=P)
                    dst = dst.rearrange("p (s c u) -> p s c u", s=2, c=P, u=2)
                else:
                    src = turned[:].rearrange("p (f u c) -> p c f u", f=2, u=2, c=P)
                    dst = dst.rearrange("p (c f u) -> p c f u", c=P, f=2, u=2)
                if vector_helps and b % 2 == 1:
                    nc.vector.tensor_copy(out=dst, in_=src)
                else:
                    nc.scalar.copy(out=dst, in_=src)
            if banks_of_unit[-1] == 3:
                load_behind(unit)

        def quantise(unit, part=0, parts=1):
            kind, i = unit
            size = WORDS // parts
            lo = WORDS * i + size * part
            nc.vector.quantize_mx(
                out=codes[kind][:, lo:lo + size].bitcast(FP8X4),
                scales=scales[kind][:, lo:lo + size],
                in_=groupeds[unit][:, 4 * size * part:4 * size * (part + 1)],
            )

        def spread_bias(n):
            spread = psum_m.tile([P, BANK], F32, tag="acc")
            for h in range(4):
                r = 4 * n + h
                nc.tensor.matmul(
                    out=spread[:, P * h:P * (h + 1)],
                    lhsT=ident_b[:, r:r + 1].to_broadcast([P, P]),
                    rhs=bias_rows[:],
                    start=True,
                    stop=True,
                )
            nc.scalar.copy(out=bias[:, BANK * n:BANK * (n + 1)], in_=spread[:])

        for unit in units[0:RAW_BUFS]:
            load(unit)
            if unit == units[0]:
                for i, b in enumerate((bk, bv)):
                    nc.sync.dma_start(out=bias_rows[8 * i:8 * i + 8, :], in_=b.rearrange("(h d) -> h d", d=P))
        transpose(units[0], range(4), True)
        spread_bias(0)
        quantise(units[0])
        for half in range(2):
            transpose(units[1], (2 * half, 2 * half + 1), True)
            quantise(units[1], half, 2)
        spread_bias(1)

        totals = {}
        means = {}

        def mean_tile(n):
            if n not in means:
                means[n] = mean_pool.tile([P, 4, 4, P], F32, name="mean")
            return means[n]

        def scale(r):
            n, q = rounds[r]
            nc.scalar.activation(out=mean_tile(n)[:, :, q, :], in_=totals[r][:], func=COPY, scale=0.25)
            if r == max(s for s in range(ROUNDS) if rounds[s][0] == n and not summed_on_vector(s)):
                nc.scalar.dma_start(
                    out=mean_views[n // 2][:, 4 * (n % 2):4 * (n % 2) + 4, :],
                    in_=means[n][:].rearrange("p h q d -> p h (q d)"),
                )

        waiting = []
        scaled = 0
        for r in range(ROUNDS):
            n, q = rounds[r]
            fresh = None
            for unit in units[2:]:
                if r == prepared_in[unit]:
                    fresh = unit
            if r in (5, 9):
                spread_bias(r // 4 + 1)
            banks = []
            for t in range(4):
                if fresh is not None and t == 0:
                    transpose(fresh, range(4), False)
                acc = psum_m.tile([P, BANK], F32)
                for s in range(2):
                    xo = WORDS * q + 2 * P * t + P * s
                    wo = WORDS * n + BANK * s
                    nc.tensor.matmul_mx(
                        out=acc[:],
                        lhsT=codes["x"][:, xo:xo + P].bitcast(FP8X4),
                        lhsT_scale=scales["x"][:, xo:xo + P],
                        rhs=codes["w"][:, wo:wo + BANK].bitcast(FP8X4),
                        rhs_scale=scales["w"][:, wo:wo + BANK],
                        start=(s == 0),
                        stop=(s == 1),
                    )
                banks.append(acc[:].rearrange("p (h d) -> p h d", h=4))
            o = out_pool.tile([P, 4, 4, P], F32)
            bias_n = bias[:, BANK * n:BANK * (n + 1)].rearrange("p (h d) -> p h d", h=4)
            if summed_on_vector(r):
                run = run_pool.tile([P, 4, P], F32)

            def add_bias(t):
                nc.vector.tensor_tensor(out=o[:, :, t, :], in0=banks[t], in1=bias_n, op=ADD)

            def add_to_mean(t):
                nc.vector.scalar_tensor_tensor(
                    out=(mean_tile(n)[:, :, q, :] if t == 3 else run[:]),
                    in0=banks[t],
                    scalar=0.25,
                    in1=(bias_n if t == 0 else run[:]),
                    op0=MULT,
                    op1=ADD,
                )

            behind = 1 if r == ROUNDS - 1 else 0
            for t in range(4 + behind):
                if t < 4:
                    add_bias(t)
                if summed_on_vector(r) and t >= behind:
                    add_to_mean(t - behind)
                if t == 1 and fresh is not None:
                    quantise(fresh)
            nc.sync.dma_start(
                out=kv_views[n // 2][:, 4 * (n % 2):4 * (n % 2) + 4, BANK * q:BANK * (q + 1)],
                in_=o[:].rearrange("p h j d -> p h (j d)"),
            )
            if not summed_on_vector(r):
                half = half_pool.tile([P, 4, 2, P], F32)
                nc.gpsimd.tensor_tensor(out=half[:], in0=o[:, :, 0:2, :], in1=o[:, :, 2:4, :], op=ADD)
                total = total_pool.tile([P, 4, P], F32)
                nc.gpsimd.tensor_tensor(out=total[:], in0=half[:, :, 0, :], in1=half[:, :, 1, :], op=ADD)
                totals[r] = total
                waiting.append(r)
            while scaled < len(waiting) and (waiting[scaled] + SCALE_LAG <= r or r == ROUNDS - 1):
                scale(waiting[scaled])
                scaled += 1
